import numpy as np
import ml_dtypes


def mxq(x, axis, fmt="e4m3"):
    dtype, down = {"e4m3": (ml_dtypes.float8_e4m3fn, 7), "e5m2": (ml_dtypes.float8_e5m2, 14)}[fmt]
    v = np.moveaxis(np.asarray(x, np.float32).astype(ml_dtypes.bfloat16).astype(np.float64), axis, -1)
    blocks = v.reshape(v.shape[:-1] + (-1, 32))
    amax = np.abs(blocks).max(-1, keepdims=True)
    byte = np.maximum(np.where(amax > 0, np.frexp(amax)[1] - 1 + 127, 0) - down, 1)
    scale = np.exp2(byte - 127.0)
    codes = (blocks / scale).astype(np.float32).astype(dtype).astype(np.float64)
    return np.moveaxis((codes * scale).reshape(v.shape), -1, axis)


WIDE = False


def mx_kscale(k):
    if not WIDE:
        return np.ones(k)
    levels = np.array([10, -10, 5, -5, 0])
    a = np.random.permutation(np.resize(levels, k // 512 * 4)).reshape(k // 512, 4)
    idx = np.arange(k)
    return np.exp2(a[idx // 512, idx % 128 // 32])


BF16 = ml_dtypes.bfloat16


def bf(x):
    return np.asarray(x, np.float32).astype(BF16)


def f64(x):
    return np.asarray(x).astype(np.float64)


B, S, IN_DIM, OUT_DIM, MOD_DIM = 4, 512, 512, 512, 512
EPS = 1e-8
GAIN = np.sqrt(2.0 / (1.0 + 0.2 ** 2))


def setup_inputs():
    ks = mx_kscale(MOD_DIM)
    kt = mx_kscale(IN_DIM)
    return {"x": bf(np.random.standard_normal((B, S, IN_DIM))),
            "modulation": bf(np.random.standard_normal((B, S, MOD_DIM)) * ks),
            "weight": bf(np.random.standard_normal((OUT_DIM, IN_DIM)) * GAIN / np.sqrt(IN_DIM) / kt[None, :]),
            "bias": bf(np.random.standard_normal(OUT_DIM) * 0.1),
            "mod_w": bf(np.random.standard_normal((IN_DIM, MOD_DIM)) / np.sqrt(MOD_DIM) * kt[:, None] / ks[None, :]),
            "mod_b": bf((1.0 + 0.1 * np.random.standard_normal(IN_DIM)) * kt)}


def reference(x, modulation, weight, bias, mod_w, mod_b):
    xf, w = f64(x), f64(weight)
    s = (mxq(f64(modulation), 2, "e4m3") @ mxq(f64(mod_w), 1, "e4m3").T) + f64(mod_b)
    out = mxq(xf * s, 2, "e4m3") @ mxq(w, 1, "e4m3").T
    demod = 1.0 / np.sqrt((mxq(s * s, 2, "e4m3") @ mxq(w * w, 1, "e4m3").T) + EPS)
    return out * demod + f64(bias)

@@ -1,0 +1,313 @@
+from contextlib import ExitStack
+
+import concourse.mybir as mybir
+from concourse.masks import make_identity
+
+F32 = mybir.dt.float32
+BF16 = mybir.dt.bfloat16
+U32 = mybir.dt.uint32
+U8 = mybir.dt.uint8
+FP8X4 = mybir.dt.float8_e4m3fn_x4
+ACT = mybir.ActivationFunctionType
+ALU = mybir.AluOpType
+
+P = 128
+DIM = 512
+NT = 16
+NU = 8
+FLOPS = 3 * 2 * 2048 * 512 * 512
+
+MANUAL = True
+ADD_G = ()
+SS_V = ()
+CMOD_V = ()
+LEAD = 3
+
+
+def tile_modulatedlinear_kernel(tc, x, modulation, weight, bias, mod_w, mod_b, out):
+    nc = tc.nc
+    with ExitStack() as ctx:
+        const = ctx.enter_context(tc.tile_pool(name="const", bufs=1))
+        work = ctx.enter_context(tc.tile_pool(name="work", bufs=2))
+        psum = ctx.enter_context(tc.psum_pool(name="psum", bufs=1))
+        if MANUAL:
+            ctx.enter_context(tc.manual_schedule())
+
+        xv = x.flatten_outer_dims().rearrange("(p j) i -> p j i", j=NT)
+        mv = modulation.flatten_outer_dims().rearrange("(p j) i -> p j i", j=NT)
+        ov = out.flatten_outer_dims().rearrange("(p j) o -> p j o", j=NT)
+        mwv = mod_w.rearrange("(u p e) m -> p u e m", u=2, e=2)
+
+        x_sb = const.tile([P, NT, DIM], BF16, name="x_sb")
+        m_sb = const.tile([P, NT, DIM], BF16, name="m_sb")
+        mw_sb = const.tile([P, 4, DIM], BF16, name="mw_sb")
+        w_sb = const.tile([P, 4, DIM], BF16, name="w_sb")
+        mb_raw = const.tile([P, 4], BF16, name="mb_raw")
+        brow = const.tile([P, DIM], BF16, name="brow")
+        ones = const.tile([P, P], BF16, name="ones")
+        ident = const.tile([P, P], F32, name="ident")
+
+        make_identity(nc, ident[:])
+        nc.vector.memset(brow[:], 0.0)
+        nc.vector.memset(ones[:], 1.0)
+
+        def load_m(lo, hi):
+            nc.sync.dma_start(out=m_sb[:, lo:hi, :], in_=mv[:, lo:hi, :])
+
+        def load_x(lo, hi):
+            nc.sync.dma_start(out=x_sb[:, lo:hi, :], in_=xv[:, lo:hi, :])
+
+        load_m(0, 2)
+        for u in range(2):
+            nc.sync.dma_start(out=mw_sb[:, 2 * u:2 * u + 2, :], in_=mwv[:, u, :, :])
+        nc.scalar.dma_start(
+            out=mb_raw[:].rearrange("p (u e) -> p u e", u=2),
+            in_=mod_b.rearrange("(u p e) -> p u e", u=2, e=2),
+        )
+        nc.scalar.dma_start(out=brow[0:1, :], in_=bias.rearrange("(a n) -> a n", a=1))
+        load_m(2, 4)
+        nc.sync.dma_start(out=w_sb[:], in_=weight.rearrange("(c p) i -> p c i", p=P))
+        load_x(0, 2)
+        load_m(4, 8)
+        load_x(2, 4)
+        load_x(4, 8)
+        load_m(8, 16)
+        load_x(8, 16)
+
+        def bank(tag):
+            return psum.tile([P, 512], F32, name=tag, tag=tag)
+
+        modb = const.tile([P, 4], F32, name="modb")
+        mwg = const.tile([P, 2048], BF16, name="mwg", align_bytes=64)
+        mw_codes = const.tile([P, 512], U32, name="mw_codes", align_bytes=64)
+        mw_scales = const.tile([P, 512], U8, name="mw_scales", align_bytes=64)
+        wg = const.tile([P, 2048], BF16, name="wg", align_bytes=64)
+        w2g = const.tile([P, 2048], BF16, name="w2g", align_bytes=64)
+        w_codes = const.tile([P, 512], U32, name="w_codes", align_bytes=64)
+        w_scales = const.tile([P, 512], U8, name="w_scales", align_bytes=64)
+        w2_codes = const.tile([P, 512], U32, name="w2_codes", align_bytes=64)
+        w2_scales = const.tile([P, 512], U8, name="w2_scales", align_bytes=64)
+        bias_bc = const.tile([P, DIM], F32, name="bias_bc")
+
+        T = {}
+
+        def copy_on(vector, dst, src):
+            if vector:
+                nc.vector.tensor_copy(out=dst, in_=src)
+            else:
+                nc.scalar.copy(out=dst, in_=src)
+
+        def mw_transposes(b):
+            t = bank(("y0", "q0")[b])
+            for c2 in range(2):
+                words = mw_sb[:, 2 * b + c2, :].bitcast(F32)
+                for v in range(2):
+                    col = (c2 * 2 + v) * P
+                    nc.tensor.transpose(t[:, col:col + P], words[:, v * P:(v + 1) * P], ident[:])
+            T[("mwt", b)] = t
+
+        def mw_copy(b, vector):
+            copy_on(
+                vector,
+                mwg[:].bitcast(F32)[:, b * 512:(b + 1) * 512].rearrange("p (c i v) -> p c i v", c=2, v=2),
+                T[("mwt", b)][:].rearrange("p (c v i) -> p c i v", c=2, v=2),
+            )
+
+        def mw_quant(b):
+            nc.vector.quantize_mx(
+                out=mw_codes[:, b * 256:(b + 1) * 256].bitcast(FP8X4),
+                scales=mw_scales[:, b * 256:(b + 1) * 256],
+                in_=mwg[:, b * 1024:(b + 1) * 1024],
+            )
+
+        def w_transposes():
+            wt = [bank("y1"), bank("q1")]
+            for oc in range(4):
+                words = w_sb[:, oc, :].bitcast(F32)
+                for u in range(2):
+                    col = u * 256 + (oc % 2) * P
+                    nc.tensor.transpose(wt[oc // 2][:, col:col + P], words[:, u * P:(u + 1) * P], ident[:])
+            pb = bank("y0")
+            nc.tensor.matmul(out=pb[:], lhsT=ones[:], rhs=brow[:], start=True, stop=True)
+            T["wt"] = wt
+            T["pb"] = pb
+
+        def w_rest():
+            wt = T["wt"]
+            for b in range(2):
+                nc.vector.tensor_copy(
+                    out=wg[:].bitcast(F32)[:, b * 512:(b + 1) * 512].rearrange("p (o u) -> p o u", u=2),
+                    in_=wt[b][:].rearrange("p (u o) -> p o u", u=2),
+                )
+                nc.scalar.activation(
+                    out=w2g[:, b * 1024:(b + 1) * 1024].rearrange("p (o u e) -> p o u e", u=2, e=2),
+                    in_=wt[b][:].bitcast(BF16).rearrange("p (u o e) -> p o u e", u=2, e=2),
+                    func=ACT.Square,
+                )
+            nc.vector.quantize_mx(out=w_codes[:].bitcast(FP8X4), scales=w_scales[:], in_=wg[:])
+            nc.vector.tensor_copy(out=bias_bc[:], in_=T["pb"][:])
+            nc.vector.quantize_mx(out=w2_codes[:].bitcast(FP8X4), scales=w2_scales[:], in_=w2g[:])
+
+        def transposes(src, n, tag):
+            t = bank(tag)
+            for h in range(2):
+                words = src[:, 2 * n + h, :].bitcast(F32)
+                for u in range(2):
+                    col = u * 256 + h * P
+                    nc.tensor.transpose(t[:, col:col + P], words[:, u * P:(u + 1) * P], ident[:])
+            T[(tag, n)] = t
+
+        def quant(key, n, bufs):
+            g = T[(key + "g", n)]
+            codes = work.tile([P, 256], U32, name=key + "_codes", tag=key + "_codes", bufs=bufs, align_bytes=64)
+            scales = work.tile([P, 256], U8, name=key + "_scales", tag=key + "_scales", bufs=bufs, align_bytes=64)
+            nc.vector.quantize_mx(out=codes[:].bitcast(FP8X4), scales=scales[:], in_=g[:])
+            T[(key, n)] = (codes, scales)
+
+        def cmod(n):
+            g = work.tile([P, 1024], BF16, name="mg", tag="mg", bufs=3, align_bytes=64)
+            copy_on(
+                n in CMOD_V,
+                g[:].bitcast(F32).rearrange("p (t u) -> p t u", u=2),
+                T[("mt", n)][:].rearrange("p (u t) -> p t u", u=2),
+            )
+            T[("mg", n)] = g
+
+        def s1(n):
+            codes, scales = T[("m", n)]
+            banks = (bank("sa"), bank("sb"))
+            for c in range(4):
+                nc.tensor.matmul_mx(
+                    out=banks[c // 2][:, (c % 2) * 256:(c % 2) * 256 + 256],
+                    lhsT=mw_codes[:, c * P:(c + 1) * P].bitcast(FP8X4),
+                    lhsT_scale=mw_scales[:, c * P:(c + 1) * P],
+                    rhs=codes[:].bitcast(FP8X4),
+                    rhs_scale=scales[:],
+                    start=True,
+                    stop=True,
+                )
+            T[("sp", n)] = banks
+
+        def sout(n):
+            banks = T[("sp", n)]
+            s = work.tile([P, 4, 256], F32, name="s_cm", tag="s_cm")
+            for c in range(4):
+                nc.scalar.activation(
+                    out=s[:, c, :],
+                    in_=banks[c // 2][:, (c % 2) * 256:(c % 2) * 256 + 256],
+                    func=ACT.Identity,
+                    bias=modb[:, c:c + 1],
+                    scale=1.0,
+                )
+            T[("s", n)] = s
+
+        def xs(n):
+            g = work.tile([P, 1024], BF16, name="xsg", tag="xsg", align_bytes=64)
+            nc.vector.tensor_tensor(
+                out=g[:].rearrange("p (t u e) -> p t u e", u=2, e=2),
+                in0=T[("s", n)][:].rearrange("p (u e) t -> p t u e", u=2),
+                in1=T[("xt", n)][:].bitcast(BF16).rearrange("p (u t e) -> p t u e", u=2, e=2),
+                op=ALU.mult,
+            )
+            T[("xsg", n)] = g
+
+        def ss(n):
+            g = work.tile([P, 1024], BF16, name="ssg", tag="ssg", align_bytes=64)
+            sv = T[("s", n)][:].rearrange("p c t -> p t c")
+            gv = g[:].rearrange("p (t c) -> p t c", c=4)
+            if n in SS_V:
+                nc.vector.tensor_tensor(out=gv, in0=sv, in1=sv, op=ALU.mult)
+            else:
+                nc.scalar.activation(out=gv, in_=sv, func=ACT.Square)
+            T[("ssg", n)] = g
+
+        def s2(n):
+            xc, xsc = T[("xs", n)]
+            sc, ssc = T[("ss", n)]
+            for h in range(2):
+                q = bank("q%d" % h)
+                y = bank("y%d" % h)
+                cols = slice(h * P, (h + 1) * P)
+                nc.tensor.matmul_mx(
+                    out=q[:], lhsT=sc[:, cols].bitcast(FP8X4), lhsT_scale=ssc[:, cols],
+                    rhs=w2_codes[:].bitcast(FP8X4), rhs_scale=w2_scales[:], start=True, stop=True,
+                )
+                nc.tensor.matmul_mx(
+                    out=y[:], lhsT=xc[:, cols].bitcast(FP8X4), lhsT_scale=xsc[:, cols],
+                    rhs=w_codes[:].bitcast(FP8X4), rhs_scale=w_scales[:], start=True, stop=True,
+                )
+                T[("q", n, h)] = q
+                T[("y", n, h)] = y
+
+        def rs_mul(n):
+            d = work.tile([P, 2, DIM], F32, name="d", tag="d")
+            z = work.tile([P, 2, DIM], F32, name="z", tag="z", bufs=3)
+            for h in range(2):
+                nc.scalar.activation(out=d[:, h, :], in_=T[("q", n, h)][:], func=ACT.Abs_reciprocal_sqrt, bias=1e-8, scale=1.0)
+                nc.vector.tensor_tensor(out=z[:, h, :], in0=T[("y", n, h)][:], in1=d[:, h, :], op=ALU.mult)
+            T[("z", n)] = z
+
+        def add_store(n):
+            z = T[("z", n)]
+            o = work.tile([P, 2, DIM], F32, name="o", tag="o", bufs=3)
+            eng = nc.gpsimd if n in ADD_G else nc.vector
+            if n == NU - 1 or n in ADD_G:
+                for h in range(2):
+                    eng.tensor_tensor(out=o[:, h, :], in0=z[:, h, :], in1=bias_bc[:], op=ALU.add)
+                    if n == NU - 1:
+                        nc.sync.dma_start(out=ov[:, 2 * n + h, :], in_=o[:, h, :])
+            else:
+                eng.tensor_tensor(out=o[:], in0=z[:], in1=bias_bc[:].unsqueeze(1).to_broadcast([P, 2, DIM]), op=ALU.add)
+            if n < NU - 1:
+                nc.sync.dma_start(out=ov[:, 2 * n:2 * n + 2, :], in_=o[:])
+
+        def ok(n):
+            return 0 <= n < NU
+
+        transposes(m_sb, 0, "mt")
+        mw_transposes(0)
+        mw_transposes(1)
+        cmod(0)
+        transposes(m_sb, 1, "mt")
+        mw_copy(0, True)
+        mw_copy(1, False)
+        quant("m", 0, LEAD + 1)
+        mw_quant(0)
+        mw_quant(1)
+        nc.vector.tensor_copy(out=modb[:], in_=mb_raw[:])
+        s1(0)
+        for n in range(1, LEAD - 1):
+            cmod(n)
+            transposes(m_sb, n + 1, "mt")
+            quant("m", n, LEAD + 1)
+        transposes(x_sb, 0, "xt")
+        w_transposes()
+        for k in range(-1, NU + 1):
+            if ok(k + 1):
+                sout(k + 1)
+            if ok(k):
+                s2(k)
+            if ok(k + 2):
+                s1(k + 2)
+            if ok(k + 1):
+                xs(k + 1)
+            if ok(k + 2):
+                transposes(x_sb, k + 2, "xt")
+            if ok(k + 1):
+                ss(k + 1)
+            if k == -1:
+                w_rest()
+            if ok(k - 1) and (k - 1) not in ADD_G:
+                add_store(k - 1)
+            if ok(k + LEAD):
+                cmod(k + LEAD)
+                if ok(k + LEAD + 1):
+                    transposes(m_sb, k + LEAD + 1, "mt")
+                quant("m", k + LEAD, LEAD + 1)
+            if ok(k + 1):
+                quant("ss", k + 1, 3)
+                quant("xs", k + 1, 3)
+            if ok(k):
+                rs_mul(k)
+                if k in ADD_G:
+                    add_store(k)

@@ -18,9 +18,9 @@ NU = 8
 FLOPS = 3 * 2 * 2048 * 512 * 512
 
 MANUAL = True
-ADD_G = ()
-SS_V = ()
-CMOD_V = ()
+ADD_G = (0, 1, 2, 3, 4, 5, 6)
+SS_V = (1, 3, 5)
+CMOD_V = (4, 6)
 LEAD = 3
 
 
@@ -213,8 +213,8 @@ def tile_modulatedlinear_kernel(tc, x, modulation, weight, bias, mod_w, mod_b, o
 
         def ss(n):
             g = work.tile([P, 1024], BF16, name="ssg", tag="ssg", align_bytes=64)
-            sv = T[("s", n)][:].rearrange("p c t -> p t c")
-            gv = g[:].rearrange("p (t c) -> p t c", c=4)
+            sv = T[("s", n)][:].rearrange("p c (b i) -> p b c i", i=4)
+            gv = g[:].rearrange("p (b i c) -> p b c i", i=4, c=4)
             if n in SS_V:
                 nc.vector.tensor_tensor(out=gv, in0=sv, in1=sv, op=ALU.mult)
             else:

@@ -18,10 +18,8 @@ NU = 8
 FLOPS = 3 * 2 * 2048 * 512 * 512
 
 MANUAL = True
-ADD_G = (0, 1, 2, 3, 4, 5, 6)
-SS_V = (1, 3, 5)
-CMOD_V = (4, 6)
-LEAD = 3
+ADD_V = (7,)
+CMOD_S = (0,)
 
 
 def tile_modulatedlinear_kernel(tc, x, modulation, weight, bias, mod_w, mod_b, out):
@@ -46,7 +44,9 @@ def tile_modulatedlinear_kernel(tc, x, modulation, weight, bias, mod_w, mod_b, o
         brow = const.tile([P, DIM], BF16, name="brow")
         ones = const.tile([P, P], BF16, name="ones")
         ident = const.tile([P, P], F32, name="ident")
+        warm = const.tile([P, 1], F32, name="warm")
 
+        nc.vector.memset(warm[:], 1.0)
         make_identity(nc, ident[:])
         nc.vector.memset(brow[:], 0.0)
         nc.vector.memset(ones[:], 1.0)
@@ -65,11 +65,12 @@ def tile_modulatedlinear_kernel(tc, x, modulation, weight, bias, mod_w, mod_b, o
             in_=mod_b.rearrange("(u p e) -> p u e", u=2, e=2),
         )
         nc.scalar.dma_start(out=brow[0:1, :], in_=bias.rearrange("(a n) -> a n", a=1))
-        load_m(2, 4)
+        nc.scalar.activation(out=warm[:], in_=warm[:], func=ACT.Abs_reciprocal_sqrt, bias=1e-8, scale=1.0)
         nc.sync.dma_start(out=w_sb[:], in_=weight.rearrange("(c p) i -> p c i", p=P))
         load_x(0, 2)
-        load_m(4, 8)
+        load_m(2, 4)
         load_x(2, 4)
+        load_m(4, 8)
         load_x(4, 8)
         load_m(8, 16)
         load_x(8, 16)
@@ -127,26 +128,23 @@ def tile_modulatedlinear_kernel(tc, x, modulation, weight, bias, mod_w, mod_b, o
                 for u in range(2):
                     col = u * 256 + (oc % 2) * P
                     nc.tensor.transpose(wt[oc // 2][:, col:col + P], words[:, u * P:(u + 1) * P], ident[:])
+            T["wt"] = wt
+
+        def w_copy(b, vector):
+            copy_on(
+                vector,
+                wg[:].bitcast(F32)[:, b * 512:(b + 1) * 512].rearrange("p (o u) -> p o u", u=2),
+                T["wt"][b][:].rearrange("p (u o) -> p o u", u=2),
+            )
+
+        def w_square(b):
+            half = slice(b * 1024, (b + 1) * 1024)
+            nc.vector.tensor_tensor(out=w2g[:, half], in0=wg[:, half], in1=wg[:, half], op=ALU.mult)
+
+        def bias_matmul():
             pb = bank("y0")
             nc.tensor.matmul(out=pb[:], lhsT=ones[:], rhs=brow[:], start=True, stop=True)
-            T["wt"] = wt
             T["pb"] = pb
-
-        def w_rest():
-            wt = T["wt"]
-            for b in range(2):
-                nc.vector.tensor_copy(
-                    out=wg[:].bitcast(F32)[:, b * 512:(b + 1) * 512].rearrange("p (o u) -> p o u", u=2),
-                    in_=wt[b][:].rearrange("p (u o) -> p o u", u=2),
-                )
-                nc.scalar.activation(
-                    out=w2g[:, b * 1024:(b + 1) * 1024].rearrange("p (o u e) -> p o u e", u=2, e=2),
-                    in_=wt[b][:].bitcast(BF16).rearrange("p (u o e) -> p o u e", u=2, e=2),
-                    func=ACT.Square,
-                )
-            nc.vector.quantize_mx(out=w_codes[:].bitcast(FP8X4), scales=w_scales[:], in_=wg[:])
-            nc.vector.tensor_copy(out=bias_bc[:], in_=T["pb"][:])
-            nc.vector.quantize_mx(out=w2_codes[:].bitcast(FP8X4), scales=w2_scales[:], in_=w2g[:])
 
         def transposes(src, n, tag):
             t = bank(tag)
@@ -157,21 +155,26 @@ def tile_modulatedlinear_kernel(tc, x, modulation, weight, bias, mod_w, mod_b, o
                     nc.tensor.transpose(t[:, col:col + P], words[:, u * P:(u + 1) * P], ident[:])
             T[(tag, n)] = t
 
-        def quant(key, n, bufs):
-            g = T[(key + "g", n)]
-            codes = work.tile([P, 256], U32, name=key + "_codes", tag=key + "_codes", bufs=bufs, align_bytes=64)
-            scales = work.tile([P, 256], U8, name=key + "_scales", tag=key + "_scales", bufs=bufs, align_bytes=64)
-            nc.vector.quantize_mx(out=codes[:].bitcast(FP8X4), scales=scales[:], in_=g[:])
-            T[(key, n)] = (codes, scales)
+        def tmod(n):
+            transposes(m_sb, n, "mt")
+
+        def tx(n):
+            transposes(x_sb, n, "xt")
 
         def cmod(n):
             g = work.tile([P, 1024], BF16, name="mg", tag="mg", bufs=3, align_bytes=64)
             copy_on(
-                n in CMOD_V,
+                n not in CMOD_S,
                 g[:].bitcast(F32).rearrange("p (t u) -> p t u", u=2),
                 T[("mt", n)][:].rearrange("p (u t) -> p t u", u=2),
             )
             T[("mg", n)] = g
+
+        def qm(n):
+            codes = work.tile([P, 256], U32, name="m_codes", tag="m_codes", bufs=3, align_bytes=64)
+            scales = work.tile([P, 256], U8, name="m_scales", tag="m_scales", bufs=3, align_bytes=64)
+            nc.vector.quantize_mx(out=codes[:].bitcast(FP8X4), scales=scales[:], in_=T[("mg", n)][:])
+            T[("m", n)] = (codes, scales)
 
         def s1(n):
             codes, scales = T[("m", n)]
@@ -200,114 +203,122 @@ def tile_modulatedlinear_kernel(tc, x, modulation, weight, bias, mod_w, mod_b, o
                     scale=1.0,
                 )
             T[("s", n)] = s
+            T[("g", n)] = work.tile([P, 2048], BF16, name="g2", tag="g2", bufs=3, align_bytes=64)
 
         def xs(n):
-            g = work.tile([P, 1024], BF16, name="xsg", tag="xsg", align_bytes=64)
             nc.vector.tensor_tensor(
-                out=g[:].rearrange("p (t u e) -> p t u e", u=2, e=2),
+                out=T[("g", n)][:, 0:1024].rearrange("p (t u e) -> p t u e", u=2, e=2),
                 in0=T[("s", n)][:].rearrange("p (u e) t -> p t u e", u=2),
                 in1=T[("xt", n)][:].bitcast(BF16).rearrange("p (u t e) -> p t u e", u=2, e=2),
                 op=ALU.mult,
             )
-            T[("xsg", n)] = g
 
         def ss(n):
-            g = work.tile([P, 1024], BF16, name="ssg", tag="ssg", align_bytes=64)
             sv = T[("s", n)][:].rearrange("p c (b i) -> p b c i", i=4)
-            gv = g[:].rearrange("p (b i c) -> p b c i", i=4, c=4)
-            if n in SS_V:
-                nc.vector.tensor_tensor(out=gv, in0=sv, in1=sv, op=ALU.mult)
-            else:
-                nc.scalar.activation(out=gv, in_=sv, func=ACT.Square)
-            T[("ssg", n)] = g
+            gv = T[("g", n)][:, 1024:2048].rearrange("p (b i c) -> p b c i", i=4, c=4)
+            nc.scalar.activation(out=gv, in_=sv, func=ACT.Square)
 
-        def s2(n):
-            xc, xsc = T[("xs", n)]
-            sc, ssc = T[("ss", n)]
-            for h in range(2):
-                q = bank("q%d" % h)
-                y = bank("y%d" % h)
-                cols = slice(h * P, (h + 1) * P)
-                nc.tensor.matmul_mx(
-                    out=q[:], lhsT=sc[:, cols].bitcast(FP8X4), lhsT_scale=ssc[:, cols],
-                    rhs=w2_codes[:].bitcast(FP8X4), rhs_scale=w2_scales[:], start=True, stop=True,
-                )
-                nc.tensor.matmul_mx(
-                    out=y[:], lhsT=xc[:, cols].bitcast(FP8X4), lhsT_scale=xsc[:, cols],
-                    rhs=w_codes[:].bitcast(FP8X4), rhs_scale=w_scales[:], start=True, stop=True,
-                )
-                T[("q", n, h)] = q
-                T[("y", n, h)] = y
+        def quant2(n):
+            codes = work.tile([P, 512], U32, name="g_codes", tag="g_codes", bufs=3, align_bytes=64)
+            scales = work.tile([P, 512], U8, name="g_scales", tag="g_scales", bufs=3, align_bytes=64)
+            nc.vector.quantize_mx(out=codes[:].bitcast(FP8X4), scales=scales[:], in_=T[("g", n)][:])
+            T[("c", n)] = (codes, scales)
 
-        def rs_mul(n):
+        def s2(n, h, which):
+            codes, scales = T[("c", n)]
+            t = bank(which + "%d" % h)
+            lo = (256 if which == "q" else 0) + h * P
+            nc.tensor.matmul_mx(
+                out=t[:],
+                lhsT=codes[:, lo:lo + P].bitcast(FP8X4),
+                lhsT_scale=scales[:, lo:lo + P],
+                rhs=(w2_codes if which == "q" else w_codes)[:].bitcast(FP8X4),
+                rhs_scale=(w2_scales if which == "q" else w_scales)[:],
+                start=True,
+                stop=True,
+            )
+            T[(which, n, h)] = t
+
+        def rs(n):
             d = work.tile([P, 2, DIM], F32, name="d", tag="d")
-            z = work.tile([P, 2, DIM], F32, name="z", tag="z", bufs=3)
             for h in range(2):
                 nc.scalar.activation(out=d[:, h, :], in_=T[("q", n, h)][:], func=ACT.Abs_reciprocal_sqrt, bias=1e-8, scale=1.0)
-                nc.vector.tensor_tensor(out=z[:, h, :], in0=T[("y", n, h)][:], in1=d[:, h, :], op=ALU.mult)
-            T[("z", n)] = z
+            T[("d", n)] = d
+            T[("z", n)] = work.tile([P, 2, DIM], F32, name="z", tag="z", bufs=3)
+            T[("o", n)] = work.tile([P, 2, DIM], F32, name="o", tag="o", bufs=3)
 
-        def add_store(n):
+        def mul_add(n, h):
             z = T[("z", n)]
-            o = work.tile([P, 2, DIM], F32, name="o", tag="o", bufs=3)
-            eng = nc.gpsimd if n in ADD_G else nc.vector
-            if n == NU - 1 or n in ADD_G:
-                for h in range(2):
-                    eng.tensor_tensor(out=o[:, h, :], in0=z[:, h, :], in1=bias_bc[:], op=ALU.add)
-                    if n == NU - 1:
-                        nc.sync.dma_start(out=ov[:, 2 * n + h, :], in_=o[:, h, :])
-            else:
-                eng.tensor_tensor(out=o[:], in0=z[:], in1=bias_bc[:].unsqueeze(1).to_broadcast([P, 2, DIM]), op=ALU.add)
-            if n < NU - 1:
-                nc.sync.dma_start(out=ov[:, 2 * n:2 * n + 2, :], in_=o[:])
+            o = T[("o", n)]
+            nc.vector.tensor_tensor(out=z[:, h, :], in0=T[("y", n, h)][:], in1=T[("d", n)][:, h, :], op=ALU.mult)
+            eng = nc.vector if n in ADD_V else nc.gpsimd
+            eng.tensor_tensor(out=o[:, h, :], in0=z[:, h, :], in1=bias_bc[:], op=ALU.add)
+            if n == NU - 1:
+                nc.sync.dma_start(out=ov[:, 2 * n + h, :], in_=o[:, h, :])
 
         def ok(n):
             return 0 <= n < NU
 
-        transposes(m_sb, 0, "mt")
+        tmod(0)
         mw_transposes(0)
         mw_transposes(1)
         cmod(0)
-        transposes(m_sb, 1, "mt")
         mw_copy(0, True)
         mw_copy(1, False)
-        quant("m", 0, LEAD + 1)
+        qm(0)
         mw_quant(0)
         mw_quant(1)
         nc.vector.tensor_copy(out=modb[:], in_=mb_raw[:])
-        s1(0)
-        for n in range(1, LEAD - 1):
-            cmod(n)
-            transposes(m_sb, n + 1, "mt")
-            quant("m", n, LEAD + 1)
-        transposes(x_sb, 0, "xt")
         w_transposes()
-        for k in range(-1, NU + 1):
-            if ok(k + 1):
-                sout(k + 1)
+        s1(0)
+        tx(0)
+        tmod(1)
+        w_copy(0, True)
+        w_copy(1, False)
+        sout(0)
+        w_square(0)
+        cmod(1)
+        tmod(2)
+        w_square(1)
+        qm(1)
+        nc.vector.quantize_mx(out=w_codes[:].bitcast(FP8X4), scales=w_scales[:], in_=wg[:])
+        nc.vector.quantize_mx(out=w2_codes[:].bitcast(FP8X4), scales=w2_scales[:], in_=w2g[:])
+        bias_matmul()
+        s1(1)
+        xs(0)
+        ss(0)
+        tx(1)
+        nc.scalar.copy(out=bias_bc[:], in_=T["pb"][:])
+        sout(1)
+        cmod(2)
+        tmod(3)
+        qm(2)
+        for k in range(-1, NU):
             if ok(k):
-                s2(k)
+                rs(k)
+            if ok(k + 1):
+                quant2(k + 1)
+            if ok(k + 3):
+                s1(k + 3)
+            if ok(k + 1):
+                s2(k + 1, 0, "q")
+                s2(k + 1, 1, "q")
+            for h in range(2):
+                if ok(k):
+                    mul_add(k, h)
+                if ok(k + 1):
+                    s2(k + 1, h, "y")
+            if ok(k) and k < NU - 1:
+                nc.sync.dma_start(out=ov[:, 2 * k:2 * k + 2, :], in_=T[("o", k)][:])
+            if ok(k + 4):
+                cmod(k + 4)
+            if ok(k + 5):
+                tmod(k + 5)
             if ok(k + 2):
-                s1(k + 2)
-            if ok(k + 1):
-                xs(k + 1)
-            if ok(k + 2):
-                transposes(x_sb, k + 2, "xt")
-            if ok(k + 1):
-                ss(k + 1)
-            if k == -1:
-                w_rest()
-            if ok(k - 1) and (k - 1) not in ADD_G:
-                add_store(k - 1)
-            if ok(k + LEAD):
-                cmod(k + LEAD)
-                if ok(k + LEAD + 1):
-                    transposes(m_sb, k + LEAD + 1, "mt")
-                quant("m", k + LEAD, LEAD + 1)
-            if ok(k + 1):
-                quant("ss", k + 1, 3)
-                quant("xs", k + 1, 3)
-            if ok(k):
-                rs_mul(k)
-                if k in ADD_G:
-                    add_store(k)
+                ss(k + 2)
+                xs(k + 2)
+            if ok(k + 3):
+                tx(k + 3)
+                sout(k + 3)
+            if ok(k + 4):
+                qm(k + 4)

@@ -17,9 +17,9 @@ NT = 16
 NU = 8
 FLOPS = 3 * 2 * 2048 * 512 * 512
 
-MANUAL = True
-ADD_V = (7,)
-CMOD_S = (0,)
+MANUAL = False
+ADD_V = (6, 7)
+CMOD_S = (0, 2, 4, 6)
 
 
 def tile_modulatedlinear_kernel(tc, x, modulation, weight, bias, mod_w, mod_b, out):

@@ -17,9 +17,10 @@ NT = 16
 NU = 8
 FLOPS = 3 * 2 * 2048 * 512 * 512
 
-MANUAL = False
-ADD_V = (6, 7)
-CMOD_S = (0, 2, 4, 6)
+PIN_START = False
+PIN_LOOP = True
+LATE_V = ((6, 1), (7, 0), (7, 1))
+CMOD_S = (0,)
 
 
 def tile_modulatedlinear_kernel(tc, x, modulation, weight, bias, mod_w, mod_b, out):
@@ -28,7 +29,7 @@ def tile_modulatedlinear_kernel(tc, x, modulation, weight, bias, mod_w, mod_b, o
         const = ctx.enter_context(tc.tile_pool(name="const", bufs=1))
         work = ctx.enter_context(tc.tile_pool(name="work", bufs=2))
         psum = ctx.enter_context(tc.psum_pool(name="psum", bufs=1))
-        if MANUAL:
+        if PIN_START:
             ctx.enter_context(tc.manual_schedule())
 
         xv = x.flatten_outer_dims().rearrange("(p j) i -> p j i", j=NT)
@@ -67,8 +68,8 @@ def tile_modulatedlinear_kernel(tc, x, modulation, weight, bias, mod_w, mod_b, o
         nc.scalar.dma_start(out=brow[0:1, :], in_=bias.rearrange("(a n) -> a n", a=1))
         nc.scalar.activation(out=warm[:], in_=warm[:], func=ACT.Abs_reciprocal_sqrt, bias=1e-8, scale=1.0)
         nc.sync.dma_start(out=w_sb[:], in_=weight.rearrange("(c p) i -> p c i", p=P))
-        load_x(0, 2)
         load_m(2, 4)
+        load_x(0, 2)
         load_x(2, 4)
         load_m(4, 8)
         load_x(4, 8)
@@ -247,14 +248,14 @@ def tile_modulatedlinear_kernel(tc, x, modulation, weight, bias, mod_w, mod_b, o
             T[("z", n)] = work.tile([P, 2, DIM], F32, name="z", tag="z", bufs=3)
             T[("o", n)] = work.tile([P, 2, DIM], F32, name="o", tag="o", bufs=3)
 
-        def mul_add(n, h):
-            z = T[("z", n)]
-            o = T[("o", n)]
-            nc.vector.tensor_tensor(out=z[:, h, :], in0=T[("y", n, h)][:], in1=T[("d", n)][:, h, :], op=ALU.mult)
-            eng = nc.vector if n in ADD_V else nc.gpsimd
-            eng.tensor_tensor(out=o[:, h, :], in0=z[:, h, :], in1=bias_bc[:], op=ALU.add)
-            if n == NU - 1:
-                nc.sync.dma_start(out=ov[:, 2 * n + h, :], in_=o[:, h, :])
+        def mul(n, h):
+            nc.vector.tensor_tensor(out=T[("z", n)][:, h, :], in0=T[("y", n, h)][:], in1=T[("d", n)][:, h, :], op=ALU.mult)
+
+        def add(eng, n, h):
+            eng.tensor_tensor(out=T[("o", n)][:, h, :], in0=T[("z", n)][:, h, :], in1=bias_bc[:], op=ALU.add)
+
+        def store(n, lo, hi):
+            nc.sync.dma_start(out=ov[:, 2 * n + lo:2 * n + hi, :], in_=T[("o", n)][:, lo:hi, :])
 
         def ok(n):
             return 0 <= n < NU
@@ -271,8 +272,8 @@ def tile_modulatedlinear_kernel(tc, x, modulation, weight, bias, mod_w, mod_b, o
         nc.vector.tensor_copy(out=modb[:], in_=mb_raw[:])
         w_transposes()
         s1(0)
-        tx(0)
         tmod(1)
+        tx(0)
         w_copy(0, True)
         w_copy(1, False)
         sout(0)
@@ -293,6 +294,8 @@ def tile_modulatedlinear_kernel(tc, x, modulation, weight, bias, mod_w, mod_b, o
         cmod(2)
         tmod(3)
         qm(2)
+        if PIN_LOOP and not PIN_START:
+            ctx.enter_context(tc.manual_schedule())
         for k in range(-1, NU):
             if ok(k):
                 rs(k)
@@ -303,13 +306,12 @@ def tile_modulatedlinear_kernel(tc, x, modulation, weight, bias, mod_w, mod_b, o
             if ok(k + 1):
                 s2(k + 1, 0, "q")
                 s2(k + 1, 1, "q")
-            for h in range(2):
-                if ok(k):
-                    mul_add(k, h)
-                if ok(k + 1):
-                    s2(k + 1, h, "y")
-            if ok(k) and k < NU - 1:
-                nc.sync.dma_start(out=ov[:, 2 * k:2 * k + 2, :], in_=T[("o", k)][:])
+            if ok(k):
+                mul(k, 0)
+                if (k, 0) not in LATE_V:
+                    add(nc.gpsimd, k, 0)
+            if ok(k + 1):
+                s2(k + 1, 0, "y")
             if ok(k + 4):
                 cmod(k + 4)
             if ok(k + 5):
@@ -319,6 +321,21 @@ def tile_modulatedlinear_kernel(tc, x, modulation, weight, bias, mod_w, mod_b, o
                 xs(k + 2)
             if ok(k + 3):
                 tx(k + 3)
+            if ok(k):
+                mul(k, 1)
+                if (k, 1) not in LATE_V:
+                    add(nc.gpsimd, k, 1)
+            if ok(k + 1):
+                s2(k + 1, 1, "y")
+            if ok(k):
+                if (k, 0) not in LATE_V and (k, 1) not in LATE_V:
+                    store(k, 0, 2)
+                elif (k, 0) not in LATE_V:
+                    store(k, 0, 1)
+            if ok(k + 3):
                 sout(k + 3)
             if ok(k + 4):
                 qm(k + 4)
+        for n, h in LATE_V:
+            add(nc.vector, n, h)
+            store(n, h, h + 1)

@@ -17,6 +17,8 @@ NT = 16
 NU = 8
 FLOPS = 3 * 2 * 2048 * 512 * 512
 
+WARM_A = 4
+WARM_B = 2
 PIN_START = False
 PIN_LOOP = True
 LATE_V = ((6, 1), (7, 0), (7, 1))
@@ -46,11 +48,13 @@ def tile_modulatedlinear_kernel(tc, x, modulation, weight, bias, mod_w, mod_b, o
         ones = const.tile([P, P], BF16, name="ones")
         ident = const.tile([P, P], F32, name="ident")
         warm = const.tile([P, 1], F32, name="warm")
+        dz = const.tile([P, DIM], BF16, name="dz")
 
+        nc.vector.memset(ones[:], 1.0)
+        nc.vector.memset(dz[:], 0.0)
         nc.vector.memset(warm[:], 1.0)
         make_identity(nc, ident[:])
         nc.vector.memset(brow[:], 0.0)
-        nc.vector.memset(ones[:], 1.0)
 
         def load_m(lo, hi):
             nc.sync.dma_start(out=m_sb[:, lo:hi, :], in_=mv[:, lo:hi, :])
@@ -260,11 +264,18 @@ def tile_modulatedlinear_kernel(tc, x, modulation, weight, bias, mod_w, mod_b, o
         def ok(n):
             return 0 <= n < NU
 
+        def idle_matmuls(count, tag, rhs):
+            t = bank(tag)
+            for i in range(count):
+                nc.tensor.matmul(out=t[:], lhsT=ones[:], rhs=rhs, start=True, stop=True)
+
+        idle_matmuls(WARM_A, "sa", dz[:])
         tmod(0)
         mw_transposes(0)
         mw_transposes(1)
         cmod(0)
         mw_copy(0, True)
+        idle_matmuls(WARM_B, "sb", mwg[:, 0:DIM])
         mw_copy(1, False)
         qm(0)
         mw_quant(0)

@@ -17,7 +17,7 @@ NT = 16
 NU = 8
 FLOPS = 3 * 2 * 2048 * 512 * 512
 
-WARM_A = 4
+WARM_A = 6
 WARM_B = 2
 PIN_START = False
 PIN_LOOP = True

@@ -17,8 +17,6 @@ NT = 16
 NU = 8
 FLOPS = 3 * 2 * 2048 * 512 * 512
 
-WARM_A = 6
-WARM_B = 2
 PIN_START = False
 PIN_LOOP = True
 LATE_V = ((6, 1), (7, 0), (7, 1))
@@ -48,13 +46,11 @@ def tile_modulatedlinear_kernel(tc, x, modulation, weight, bias, mod_w, mod_b, o
         ones = const.tile([P, P], BF16, name="ones")
         ident = const.tile([P, P], F32, name="ident")
         warm = const.tile([P, 1], F32, name="warm")
-        dz = const.tile([P, DIM], BF16, name="dz")
 
-        nc.vector.memset(ones[:], 1.0)
-        nc.vector.memset(dz[:], 0.0)
         nc.vector.memset(warm[:], 1.0)
         make_identity(nc, ident[:])
         nc.vector.memset(brow[:], 0.0)
+        nc.vector.memset(ones[:], 1.0)
 
         def load_m(lo, hi):
             nc.sync.dma_start(out=m_sb[:, lo:hi, :], in_=mv[:, lo:hi, :])
@@ -264,18 +260,11 @@ def tile_modulatedlinear_kernel(tc, x, modulation, weight, bias, mod_w, mod_b, o
         def ok(n):
             return 0 <= n < NU
 
-        def idle_matmuls(count, tag, rhs):
-            t = bank(tag)
-            for i in range(count):
-                nc.tensor.matmul(out=t[:], lhsT=ones[:], rhs=rhs, start=True, stop=True)
-
-        idle_matmuls(WARM_A, "sa", dz[:])
         tmod(0)
         mw_transposes(0)
         mw_transposes(1)
         cmod(0)
         mw_copy(0, True)
-        idle_matmuls(WARM_B, "sb", mwg[:, 0:DIM])
         mw_copy(1, False)
         qm(0)
         mw_quant(0)
@@ -323,15 +312,6 @@ def tile_modulatedlinear_kernel(tc, x, modulation, weight, bias, mod_w, mod_b, o
                     add(nc.gpsimd, k, 0)
             if ok(k + 1):
                 s2(k + 1, 0, "y")
-            if ok(k + 4):
-                cmod(k + 4)
-            if ok(k + 5):
-                tmod(k + 5)
-            if ok(k + 2):
-                ss(k + 2)
-                xs(k + 2)
-            if ok(k + 3):
-                tx(k + 3)
             if ok(k):
                 mul(k, 1)
                 if (k, 1) not in LATE_V:
@@ -343,6 +323,15 @@ def tile_modulatedlinear_kernel(tc, x, modulation, weight, bias, mod_w, mod_b, o
                     store(k, 0, 2)
                 elif (k, 0) not in LATE_V:
                     store(k, 0, 1)
+            if ok(k + 4):
+                cmod(k + 4)
+            if ok(k + 5):
+                tmod(k + 5)
+            if ok(k + 2):
+                ss(k + 2)
+                xs(k + 2)
+            if ok(k + 3):
+                tx(k + 3)
             if ok(k + 3):
                 sout(k + 3)
             if ok(k + 4):

from contextlib import ExitStack

import concourse.mybir as mybir
from concourse.masks import make_identity

F32 = mybir.dt.float32
BF16 = mybir.dt.bfloat16
U32 = mybir.dt.uint32
U8 = mybir.dt.uint8
FP8X4 = mybir.dt.float8_e4m3fn_x4
ACT = mybir.ActivationFunctionType
ALU = mybir.AluOpType

P = 128
DIM = 512
NT = 16
NU = 8
FLOPS = 3 * 2 * 2048 * 512 * 512

PIN_START = False
PIN_LOOP = True
LATE_V = ((6, 1), (7, 0), (7, 1))
CMOD_S = (0,)


def tile_modulatedlinear_kernel(tc, x, modulation, weight, bias, mod_w, mod_b, out):
    nc = tc.nc
    with ExitStack() as ctx:
        const = ctx.enter_context(tc.tile_pool(name="const", bufs=1))
        work = ctx.enter_context(tc.tile_pool(name="work", bufs=2))
        psum = ctx.enter_context(tc.psum_pool(name="psum", bufs=1))
        if PIN_START:
            ctx.enter_context(tc.manual_schedule())

        xv = x.flatten_outer_dims().rearrange("(p j) i -> p j i", j=NT)
        mv = modulation.flatten_outer_dims().rearrange("(p j) i -> p j i", j=NT)
        ov = out.flatten_outer_dims().rearrange("(p j) o -> p j o", j=NT)
        mwv = mod_w.rearrange("(u p e) m -> p u e m", u=2, e=2)

        x_sb = const.tile([P, NT, DIM], BF16, name="x_sb")
        m_sb = const.tile([P, NT, DIM], BF16, name="m_sb")
        mw_sb = const.tile([P, 4, DIM], BF16, name="mw_sb")
        w_sb = const.tile([P, 4, DIM], BF16, name="w_sb")
        mb_raw = const.tile([P, 4], BF16, name="mb_raw")
        brow = const.tile([P, DIM], BF16, name="brow")
        ones = const.tile([P, P], BF16, name="ones")
        ident = const.tile([P, P], F32, name="ident")
        warm = const.tile([P, 1], F32, name="warm")

        nc.vector.memset(warm[:], 1.0)
        make_identity(nc, ident[:])
        nc.vector.memset(brow[:], 0.0)
        nc.vector.memset(ones[:], 1.0)

        def load_m(lo, hi):
            nc.sync.dma_start(out=m_sb[:, lo:hi, :], in_=mv[:, lo:hi, :])

        def load_x(lo, hi):
            nc.sync.dma_start(out=x_sb[:, lo:hi, :], in_=xv[:, lo:hi, :])

        load_m(0, 2)
        for u in range(2):
            nc.sync.dma_start(out=mw_sb[:, 2 * u:2 * u + 2, :], in_=mwv[:, u, :, :])
        nc.scalar.dma_start(
            out=mb_raw[:].rearrange("p (u e) -> p u e", u=2),
            in_=mod_b.rearrange("(u p e) -> p u e", u=2, e=2),
        )
        nc.scalar.dma_start(out=brow[0:1, :], in_=bias.rearrange("(a n) -> a n", a=1))
        nc.scalar.activation(out=warm[:], in_=warm[:], func=ACT.Abs_reciprocal_sqrt, bias=1e-8, scale=1.0)
        nc.sync.dma_start(out=w_sb[:], in_=weight.rearrange("(c p) i -> p c i", p=P))
        load_m(2, 4)
        load_x(0, 2)
        load_x(2, 4)
        load_m(4, 8)
        load_x(4, 8)
        load_m(8, 16)
        load_x(8, 16)

        def bank(tag):
            return psum.tile([P, 512], F32, name=tag, tag=tag)

        modb = const.tile([P, 4], F32, name="modb")
        mwg = const.tile([P, 2048], BF16, name="mwg", align_bytes=64)
        mw_codes = const.tile([P, 512], U32, name="mw_codes", align_bytes=64)
        mw_scales = const.tile([P, 512], U8, name="mw_scales", align_bytes=64)
        wg = const.tile([P, 2048], BF16, name="wg", align_bytes=64)
        w2g = const.tile([P, 2048], BF16, name="w2g", align_bytes=64)
        w_codes = const.tile([P, 512], U32, name="w_codes", align_bytes=64)
        w_scales = const.tile([P, 512], U8, name="w_scales", align_bytes=64)
        w2_codes = const.tile([P, 512], U32, name="w2_codes", align_bytes=64)
        w2_scales = const.tile([P, 512], U8, name="w2_scales", align_bytes=64)
        bias_bc = const.tile([P, DIM], F32, name="bias_bc")

        T = {}

        def copy_on(vector, dst, src):
            if vector:
                nc.vector.tensor_copy(out=dst, in_=src)
            else:
                nc.scalar.copy(out=dst, in_=src)

        def mw_transposes(b):
            t = bank(("y0", "q0")[b])
            for c2 in range(2):
                words = mw_sb[:, 2 * b + c2, :].bitcast(F32)
                for v in range(2):
                    col = (c2 * 2 + v) * P
                    nc.tensor.transpose(t[:, col:col + P], words[:, v * P:(v + 1) * P], ident[:])
            T[("mwt", b)] = t

        def mw_copy(b, vector):
            copy_on(
                vector,
                mwg[:].bitcast(F32)[:, b * 512:(b + 1) * 512].rearrange("p (c i v) -> p c i v", c=2, v=2),
                T[("mwt", b)][:].rearrange("p (c v i) -> p c i v", c=2, v=2),
            )

        def mw_quant(b):
            nc.vector.quantize_mx(
                out=mw_codes[:, b * 256:(b + 1) * 256].bitcast(FP8X4),
                scales=mw_scales[:, b * 256:(b + 1) * 256],
                in_=mwg[:, b * 1024:(b + 1) * 1024],
            )

        def w_transposes():
            wt = [bank("y1"), bank("q1")]
            for oc in range(4):
                words = w_sb[:, oc, :].bitcast(F32)
                for u in range(2):
                    col = u * 256 + (oc % 2) * P
                    nc.tensor.transpose(wt[oc // 2][:, col:col + P], words[:, u * P:(u + 1) * P], ident[:])
            T["wt"] = wt

        def w_copy(b, vector):
            copy_on(
                vector,
                wg[:].bitcast(F32)[:, b * 512:(b + 1) * 512].rearrange("p (o u) -> p o u", u=2),
                T["wt"][b][:].rearrange("p (u o) -> p o u", u=2),
            )

        def w_square(b):
            half = slice(b * 1024, (b + 1) * 1024)
            nc.vector.tensor_tensor(out=w2g[:, half], in0=wg[:, half], in1=wg[:, half], op=ALU.mult)

        def bias_matmul():
            pb = bank("y0")
            nc.tensor.matmul(out=pb[:], lhsT=ones[:], rhs=brow[:], start=True, stop=True)
            T["pb"] = pb

        def transposes(src, n, tag):
            t = bank(tag)
            for h in range(2):
                words = src[:, 2 * n + h, :].bitcast(F32)
                for u in range(2):
                    col = u * 256 + h * P
                    nc.tensor.transpose(t[:, col:col + P], words[:, u * P:(u + 1) * P], ident[:])
            T[(tag, n)] = t

        def tmod(n):
            transposes(m_sb, n, "mt")

        def tx(n):
            transposes(x_sb, n, "xt")

        def cmod(n):
            g = work.tile([P, 1024], BF16, name="mg", tag="mg", bufs=3, align_bytes=64)
            copy_on(
                n not in CMOD_S,
                g[:].bitcast(F32).rearrange("p (t u) -> p t u", u=2),
                T[("mt", n)][:].rearrange("p (u t) -> p t u", u=2),
            )
            T[("mg", n)] = g

        def qm(n):
            codes = work.tile([P, 256], U32, name="m_codes", tag="m_codes", bufs=3, align_bytes=64)
            scales = work.tile([P, 256], U8, name="m_scales", tag="m_scales", bufs=3, align_bytes=64)
            nc.vector.quantize_mx(out=codes[:].bitcast(FP8X4), scales=scales[:], in_=T[("mg", n)][:])
            T[("m", n)] = (codes, scales)

        def s1(n):
            codes, scales = T[("m", n)]
            banks = (bank("sa"), bank("sb"))
            for c in range(4):
                nc.tensor.matmul_mx(
                    out=banks[c // 2][:, (c % 2) * 256:(c % 2) * 256 + 256],
                    lhsT=mw_codes[:, c * P:(c + 1) * P].bitcast(FP8X4),
                    lhsT_scale=mw_scales[:, c * P:(c + 1) * P],
                    rhs=codes[:].bitcast(FP8X4),
                    rhs_scale=scales[:],
                    start=True,
                    stop=True,
                )
            T[("sp", n)] = banks

        def sout(n):
            banks = T[("sp", n)]
            s = work.tile([P, 4, 256], F32, name="s_cm", tag="s_cm")
            for c in range(4):
                nc.scalar.activation(
                    out=s[:, c, :],
                    in_=banks[c // 2][:, (c % 2) * 256:(c % 2) * 256 + 256],
                    func=ACT.Identity,
                    bias=modb[:, c:c + 1],
                    scale=1.0,
                )
            T[("s", n)] = s
            T[("g", n)] = work.tile([P, 2048], BF16, name="g2", tag="g2", bufs=3, align_bytes=64)

        def xs(n):
            nc.vector.tensor_tensor(
                out=T[("g", n)][:, 0:1024].rearrange("p (t u e) -> p t u e", u=2, e=2),
                in0=T[("s", n)][:].rearrange("p (u e) t -> p t u e", u=2),
                in1=T[("xt", n)][:].bitcast(BF16).rearrange("p (u t e) -> p t u e", u=2, e=2),
                op=ALU.mult,
            )

        def ss(n):
            sv = T[("s", n)][:].rearrange("p c (b i) -> p b c i", i=4)
            gv = T[("g", n)][:, 1024:2048].rearrange("p (b i c) -> p b c i", i=4, c=4)
            nc.scalar.activation(out=gv, in_=sv, func=ACT.Square)

        def quant2(n):
            codes = work.tile([P, 512], U32, name="g_codes", tag="g_codes", bufs=3, align_bytes=64)
            scales = work.tile([P, 512], U8, name="g_scales", tag="g_scales", bufs=3, align_bytes=64)
            nc.vector.quantize_mx(out=codes[:].bitcast(FP8X4), scales=scales[:], in_=T[("g", n)][:])
            T[("c", n)] = (codes, scales)

        def s2(n, h, which):
            codes, scales = T[("c", n)]
            t = bank(which + "%d" % h)
            lo = (256 if which == "q" else 0) + h * P
            nc.tensor.matmul_mx(
                out=t[:],
                lhsT=codes[:, lo:lo + P].bitcast(FP8X4),
                lhsT_scale=scales[:, lo:lo + P],
                rhs=(w2_codes if which == "q" else w_codes)[:].bitcast(FP8X4),
                rhs_scale=(w2_scales if which == "q" else w_scales)[:],
                start=True,
                stop=True,
            )
            T[(which, n, h)] = t

        def rs(n):
            d = work.tile([P, 2, DIM], F32, name="d", tag="d")
            for h in range(2):
                nc.scalar.activation(out=d[:, h, :], in_=T[("q", n, h)][:], func=ACT.Abs_reciprocal_sqrt, bias=1e-8, scale=1.0)
            T[("d", n)] = d
            T[("z", n)] = work.tile([P, 2, DIM], F32, name="z", tag="z", bufs=3)
            T[("o", n)] = work.tile([P, 2, DIM], F32, name="o", tag="o", bufs=3)

        def mul(n, h):
            nc.vector.tensor_tensor(out=T[("z", n)][:, h, :], in0=T[("y", n, h)][:], in1=T[("d", n)][:, h, :], op=ALU.mult)

        def add(eng, n, h):
            eng.tensor_tensor(out=T[("o", n)][:, h, :], in0=T[("z", n)][:, h, :], in1=bias_bc[:], op=ALU.add)

        def store(n, lo, hi):
            nc.sync.dma_start(out=ov[:, 2 * n + lo:2 * n + hi, :], in_=T[("o", n)][:, lo:hi, :])

        def ok(n):
            return 0 <= n < NU

        tmod(0)
        mw_transposes(0)
        mw_transposes(1)
        cmod(0)
        mw_copy(0, True)
        mw_copy(1, False)
        qm(0)
        mw_quant(0)
        mw_quant(1)
        nc.vector.tensor_copy(out=modb[:], in_=mb_raw[:])
        w_transposes()
        s1(0)
        tmod(1)
        tx(0)
        w_copy(0, True)
        w_copy(1, False)
        sout(0)
        w_square(0)
        cmod(1)
        tmod(2)
        w_square(1)
        qm(1)
        nc.vector.quantize_mx(out=w_codes[:].bitcast(FP8X4), scales=w_scales[:], in_=wg[:])
        nc.vector.quantize_mx(out=w2_codes[:].bitcast(FP8X4), scales=w2_scales[:], in_=w2g[:])
        bias_matmul()
        s1(1)
        xs(0)
        ss(0)
        tx(1)
        nc.scalar.copy(out=bias_bc[:], in_=T["pb"][:])
        sout(1)
        cmod(2)
        tmod(3)
        qm(2)
        if PIN_LOOP and not PIN_START:
            ctx.enter_context(tc.manual_schedule())
        for k in range(-1, NU):
            if ok(k):
                rs(k)
            if ok(k + 1):
                quant2(k + 1)
            if ok(k + 3):
                s1(k + 3)
            if ok(k + 1):
                s2(k + 1, 0, "q")
                s2(k + 1, 1, "q")
            if ok(k):
                mul(k, 0)
                if (k, 0) not in LATE_V:
                    add(nc.gpsimd, k, 0)
            if ok(k + 1):
                s2(k + 1, 0, "y")
            if ok(k):
                mul(k, 1)
                if (k, 1) not in LATE_V:
                    add(nc.gpsimd, k, 1)
            if ok(k + 1):
                s2(k + 1, 1, "y")
            if ok(k):
                if (k, 0) not in LATE_V and (k, 1) not in LATE_V:
                    store(k, 0, 2)
                elif (k, 0) not in LATE_V:
                    store(k, 0, 1)
            if ok(k + 4):
                cmod(k + 4)
            if ok(k + 5):
                tmod(k + 5)
            if ok(k + 2):
                ss(k + 2)
                xs(k + 2)
            if ok(k + 3):
                tx(k + 3)
            if ok(k + 3):
                sout(k + 3)
            if ok(k + 4):
                qm(k + 4)
        for n, h in LATE_V:
            add(nc.vector, n, h)
            store(n, h, h + 1)
